import numpy as np
import ml_dtypes


def mxq(x, axis, fmt="e4m3"):
    dtype, down = {"e4m3": (ml_dtypes.float8_e4m3fn, 7), "e5m2": (ml_dtypes.float8_e5m2, 14)}[fmt]
    v = np.moveaxis(np.asarray(x, np.float32).astype(ml_dtypes.bfloat16).astype(np.float64), axis, -1)
    blocks = v.reshape(v.shape[:-1] + (-1, 32))
    amax = np.abs(blocks).max(-1, keepdims=True)
    byte = np.maximum(np.where(amax > 0, np.frexp(amax)[1] - 1 + 127, 0) - down, 1)
    scale = np.exp2(byte - 127.0)
    codes = (blocks / scale).astype(np.float32).astype(dtype).astype(np.float64)
    return np.moveaxis((codes * scale).reshape(v.shape), -1, axis)


WIDE = False


def mx_kscale(k):
    if not WIDE:
        return np.ones(k)
    levels = np.array([10, -10, 5, -5, 0])
    a = np.random.permutation(np.resize(levels, k // 512 * 4)).reshape(k // 512, 4)
    idx = np.arange(k)
    return np.exp2(a[idx // 512, idx % 128 // 32])


BF16 = ml_dtypes.bfloat16


def bf(x):
    return np.asarray(x, np.float32).astype(BF16)


def f64(x):
    return np.asarray(x).astype(np.float64)


B, H, W, C, I, O, NH = 2, 16, 128, 1024, 512, 512, 8
DH = I // NH
SCALE = DH ** -0.5


def setup_inputs():
    s, t = mx_kscale(C), mx_kscale(I)
    sc = s[None, :, None, None]
    return {"left_feat": bf(np.random.standard_normal((B, C, H, W)) * sc),
            "right_feat": bf(np.random.standard_normal((B, C, H, W)) * sc),
            "wq": bf(np.random.standard_normal((I, C)) / np.sqrt(C) / s[None, :] * t[:, None]),
            "wk": bf(np.random.standard_normal((I, C)) / np.sqrt(C) / s[None, :] / t[:, None])}


def reference(left_feat, right_feat, wq, wk):
    lf = f64(left_feat).reshape(B, C, H * W)
    rf = f64(right_feat).reshape(B, C, H * W)
    q = mxq(f64(wq), 1, "e4m3") @ mxq(lf, 1, "e4m3")
    k = mxq(f64(wk), 1, "e4m3") @ mxq(rf, 1, "e4m3")
    q = q.reshape(B, I, H, W).transpose(0, 2, 3, 1)
    k = k.reshape(B, I, H, W).transpose(0, 2, 1, 3)
    return (mxq(q, 3, "e4m3") @ mxq(k, 2, "e4m3")) * SCALE

@@ -1,0 +1,253 @@
+from contextlib import ExitStack
+
+import concourse.mybir as mybir
+from concourse.masks import make_identity
+
+F32 = mybir.dt.float32
+BF16 = mybir.dt.bfloat16
+U32 = mybir.dt.uint32
+U8 = mybir.dt.uint8
+FP8X4 = mybir.dt.float8_e4m3fn_x4
+
+B, C, H, W = 2, 1024, 16, 128
+O = 512
+SCALE = 0.125
+
+P = 128
+PACK = 4
+K_PASS = P * PACK
+C_PASSES = C // K_PASS
+O_CHUNKS = O // P
+
+FLOPS = 2 * B * H * W * (2 * O * C + W * O)
+
+UNIT_ROWS = 8
+GROUP_ROWS = 4
+UNIT_COLS = UNIT_ROWS * W
+GROUP_COLS = GROUP_ROWS * W
+UNITS = [(b, half, side) for b in range(B) for half in range(H // UNIT_ROWS) for side in range(2)]
+GROUPS_PER_UNIT = UNIT_ROWS // GROUP_ROWS
+PIECES_PER_UNIT = C_PASSES * GROUPS_PER_UNIT
+N_PIECES = len(UNITS) * PIECES_PER_UNIT
+N_GROUPS = len(UNITS) * GROUPS_PER_UNIT
+N_ROWS = len(UNITS) * UNIT_ROWS
+ROWS_PER_STEP = N_ROWS // N_PIECES
+
+UNITS_AHEAD = 4
+VECTOR_COLS = 416
+
+ROW_LAG = 4
+QK_LAG = 6
+SCORE_LAG = 7
+STORE_LAG = 8
+
+
+def tile_sttm_single_pa_t_kernel(tc, left_feat, right_feat, wq, wk, out):
+    nc = tc.nc
+    feats = (left_feat, right_feat)
+    weights = (wq, wk)
+
+    with ExitStack() as ctx:
+        consts = ctx.enter_context(tc.tile_pool(name="consts", bufs=1))
+        w_stage = ctx.enter_context(tc.tile_pool(name="w_stage", bufs=2))
+        raw_pool = ctx.enter_context(tc.tile_pool(name="raw", bufs=UNITS_AHEAD * C_PASSES))
+        grouped_pool = ctx.enter_context(tc.tile_pool(name="grouped", bufs=3))
+        f_pool = ctx.enter_context(tc.tile_pool(name="f_codes", bufs=3))
+        qk_stage = ctx.enter_context(tc.tile_pool(name="qk_stage", bufs=3))
+        qk_pool = ctx.enter_context(tc.tile_pool(name="qk_codes", bufs=6))
+        res_pool = ctx.enter_context(tc.tile_pool(name="res", bufs=3))
+        acc_pool = ctx.enter_context(tc.psum_pool(name="acc", bufs=6))
+        dots_pool = ctx.enter_context(tc.psum_pool(name="dots", bufs=2))
+        ctx.enter_context(tc.manual_schedule())
+
+        raw = {}
+        w_raw = {}
+        w_grouped = {}
+        w_codes = {}
+        w_scales = {}
+        grouped = {}
+        f_codes = {}
+        f_scales = {}
+        qk_grouped = {}
+        qk_codes = {}
+        qk_scales = {}
+        dots = {}
+
+        def load_feature(unit, g):
+            b, half, side = UNITS[unit]
+            tile_raw = raw_pool.tile([P, PACK, UNIT_COLS], BF16, name="raw")
+            nc.sync.dma_start(
+                out=tile_raw[:],
+                in_=feats[side][
+                    b, g * K_PASS : (g + 1) * K_PASS, half * UNIT_ROWS : (half + 1) * UNIT_ROWS, :
+                ].rearrange("(p j) h w -> p j (h w)", j=PACK),
+            )
+            raw[(unit, g)] = tile_raw
+
+        def load_weight(side):
+            tile_w = w_stage.tile([P, O_CHUNKS * C], BF16, name="w_raw")
+            nc.sync.dma_start(
+                out=tile_w[:], in_=weights[side].rearrange("(m t) c -> m (t c)", t=O_CHUNKS)
+            )
+            w_raw[side] = tile_w
+
+        def transpose_weight(side):
+            words = w_raw[side][:].bitcast(F32).rearrange(
+                "m (t g p u) -> m t g u p", t=O_CHUNKS, g=C_PASSES, p=P, u=2
+            )
+            tile_g = w_stage.tile([P, C_PASSES * O_CHUNKS * P * PACK], BF16, name="w_grouped", align_bytes=64)
+            grouped_words = tile_g[:].bitcast(F32).rearrange(
+                "p (g t m u) -> p g t m u", g=C_PASSES, t=O_CHUNKS, m=P, u=2
+            )
+            for t in range(O_CHUNKS):
+                flipped = acc_pool.tile([P, C_PASSES, 2, P], F32, name="flipped", tag="acc")
+                for g in range(C_PASSES):
+                    for u in range(2):
+                        nc.tensor.transpose(flipped[:, g, u, :], words[:, t, g, u, :], ident[:])
+                nc.scalar.copy(
+                    out=grouped_words[:, :, t, :, :], in_=flipped[:].rearrange("p g u m -> p g m u")
+                )
+            w_grouped[side] = tile_g
+
+        def quantise_weight(side):
+            codes = consts.tile([P, C_PASSES, O_CHUNKS, P], U32, name="w_codes%d" % side, align_bytes=64)
+            scales = consts.tile([P, C_PASSES, O_CHUNKS, P], U8, name="w_scales%d" % side, align_bytes=64)
+            nc.vector.quantize_mx(
+                out=codes[:].rearrange("p g t m -> p (g t m)").bitcast(FP8X4),
+                scales=scales[:].rearrange("p g t m -> p (g t m)"),
+                in_=w_grouped[side][:],
+            )
+            w_codes[side] = codes
+            w_scales[side] = scales
+
+        def piece_place(piece):
+            unit = piece // PIECES_PER_UNIT
+            part = (piece % PIECES_PER_UNIT) // C_PASSES
+            g = piece % C_PASSES
+            return unit, g, slice(part * GROUP_COLS, (part + 1) * GROUP_COLS)
+
+        def regroup(piece):
+            unit, g, cols = piece_place(piece)
+            tile_g = grouped_pool.tile([P, GROUP_COLS, PACK], BF16, name="grouped", align_bytes=64)
+            src = raw[(unit, g)][:, :, cols]
+            for copy, share in (
+                (nc.vector.tensor_copy, slice(0, VECTOR_COLS)),
+                (nc.scalar.copy, slice(VECTOR_COLS, GROUP_COLS)),
+            ):
+                copy(
+                    out=tile_g[:, share, :].rearrange("p (c i) j -> p c j i", i=4),
+                    in_=src[:, :, share].rearrange("p j (c i) -> p c j i", i=4),
+                )
+            grouped[piece] = tile_g
+
+        def quantise(piece):
+            unit, g, cols = piece_place(piece)
+            if piece % PIECES_PER_UNIT == 0:
+                codes = f_pool.tile([P, C_PASSES, UNIT_COLS], U32, name="f_codes", align_bytes=64)
+                scales = f_pool.tile([P, C_PASSES, UNIT_COLS], U8, name="f_scales", align_bytes=64)
+                f_codes[unit] = codes
+                f_scales[unit] = scales
+            nc.vector.quantize_mx(
+                out=f_codes[unit][:, g, cols].bitcast(FP8X4),
+                scales=f_scales[unit][:, g, cols],
+                in_=grouped[piece][:].rearrange("p w j -> p (w j)"),
+            )
+
+        def project(row, copy_out):
+            unit = row // UNIT_ROWS
+            side = UNITS[unit][2]
+            group = row // GROUP_ROWS
+            cols = slice((row % UNIT_ROWS) * W, (row % UNIT_ROWS + 1) * W)
+            acc = acc_pool.tile([P, O_CHUNKS, W], F32, name="acc", tag="acc")
+            for t in range(O_CHUNKS):
+                for g in range(C_PASSES):
+                    nc.tensor.matmul_mx(
+                        out=acc[:, t, :],
+                        lhsT=w_codes[side][:, g, t, :].bitcast(FP8X4),
+                        lhsT_scale=w_scales[side][:, g, t, :],
+                        rhs=f_codes[unit][:, g, cols].bitcast(FP8X4),
+                        rhs_scale=f_scales[unit][:, g, cols],
+                        start=(g == 0),
+                        stop=(g == C_PASSES - 1),
+                    )
+            if row % GROUP_ROWS == 0:
+                tile_g = qk_stage.tile([P, GROUP_ROWS, W, O_CHUNKS], BF16, name="qk_grouped", align_bytes=64)
+                qk_grouped[group] = tile_g
+            copy_out(
+                out=qk_grouped[group][:, row % GROUP_ROWS, :, :], in_=acc[:].rearrange("p t w -> p w t")
+            )
+
+        def quantise_qk(group):
+            codes = qk_pool.tile([P, GROUP_COLS], U32, name="qk_codes", align_bytes=64)
+            scales = qk_pool.tile([P, GROUP_COLS], U8, name="qk_scales", align_bytes=64)
+            nc.vector.quantize_mx(
+                out=codes[:].bitcast(FP8X4),
+                scales=scales[:],
+                in_=qk_grouped[group][:].rearrange("p r w t -> p (r w t)"),
+            )
+            qk_codes[group] = codes
+            qk_scales[group] = scales
+
+        def multiply_scores(k_group):
+            q_group = k_group - GROUPS_PER_UNIT
+            bank = dots_pool.tile([P, GROUP_ROWS, W], F32, name="dots")
+            for r in range(GROUP_ROWS):
+                cols = slice(r * W, (r + 1) * W)
+                nc.tensor.matmul_mx(
+                    out=bank[:, r, :],
+                    lhsT=qk_codes[q_group][:, cols].bitcast(FP8X4),
+                    lhsT_scale=qk_scales[q_group][:, cols],
+                    rhs=qk_codes[k_group][:, cols].bitcast(FP8X4),
+                    rhs_scale=qk_scales[k_group][:, cols],
+                    start=True,
+                    stop=True,
+                )
+            dots[k_group] = bank
+
+        def store_scores(k_group):
+            b, half, side = UNITS[k_group // GROUPS_PER_UNIT]
+            first = half * UNIT_ROWS + (k_group % GROUPS_PER_UNIT) * GROUP_ROWS
+            res = res_pool.tile([P, GROUP_ROWS, W], F32, name="res")
+            nc.scalar.mul(out=res[:], in_=dots[k_group][:], mul=SCALE)
+            nc.sync.dma_start(
+                out=out[b, first : first + GROUP_ROWS, :, :].rearrange("h w x -> w h x"), in_=res[:]
+            )
+
+        def is_right(group):
+            return 0 <= group < N_GROUPS and UNITS[group // GROUPS_PER_UNIT][2] == 1
+
+        for unit in range(UNITS_AHEAD):
+            for g in range(C_PASSES):
+                load_feature(unit, g)
+            if unit < 2:
+                load_weight(unit)
+
+        ident = consts.tile([P, P], F32, name="ident")
+        make_identity(nc, ident[:])
+        warm = consts.tile([P, 1], F32, name="warm")
+        nc.vector.memset(warm[:], 0.0)
+        nc.scalar.mul(out=warm[:], in_=warm[:], mul=SCALE)
+
+        for k in range(N_PIECES + STORE_LAG):
+            if k < N_PIECES:
+                regroup(k)
+            if 1 <= k <= N_PIECES:
+                quantise(k - 1)
+            next_unit = k // PIECES_PER_UNIT + UNITS_AHEAD - 1
+            if k % PIECES_PER_UNIT == 0 and UNITS_AHEAD <= next_unit < len(UNITS):
+                for g in range(C_PASSES):
+                    load_feature(next_unit, g)
+            for side in range(2):
+                if k == side * PIECES_PER_UNIT + 2:
+                    transpose_weight(side)
+                if k == side * PIECES_PER_UNIT + 3:
+                    quantise_weight(side)
+            for row in range((k - ROW_LAG) * ROWS_PER_STEP, (k - ROW_LAG + 1) * ROWS_PER_STEP):
+                if 0 <= row < N_ROWS:
+                    project(row, nc.vector.tensor_copy if k > N_PIECES and row % 2 == 1 else nc.scalar.copy)
+            if (k - QK_LAG) % 2 == 0 and 0 <= (k - QK_LAG) // 2 < N_GROUPS:
+                quantise_qk((k - QK_LAG) // 2)
+            if (k - SCORE_LAG) % 2 == 0 and is_right((k - SCORE_LAG) // 2):
+                multiply_scores((k - SCORE_LAG) // 2)
+            if (k - STORE_LAG) % 2 == 0 and is_right((k - STORE_LAG) // 2):
+                store_scores((k - STORE_LAG) // 2)

@@ -34,7 +34,7 @@ N_ROWS = len(UNITS) * UNIT_ROWS
 ROWS_PER_STEP = N_ROWS // N_PIECES
 
 UNITS_AHEAD = 4
-VECTOR_COLS = 416
+VECTOR_COLS = 384
 
 ROW_LAG = 4
 QK_LAG = 6

@@ -58,7 +58,6 @@ def tile_sttm_single_pa_t_kernel(tc, left_feat, right_feat, wq, wk, out):
         res_pool = ctx.enter_context(tc.tile_pool(name="res", bufs=3))
         acc_pool = ctx.enter_context(tc.psum_pool(name="acc", bufs=6))
         dots_pool = ctx.enter_context(tc.psum_pool(name="dots", bufs=2))
-        ctx.enter_context(tc.manual_schedule())
 
         raw = {}
         w_raw = {}

@@ -34,7 +34,7 @@ N_ROWS = len(UNITS) * UNIT_ROWS
 ROWS_PER_STEP = N_ROWS // N_PIECES
 
 UNITS_AHEAD = 4
-VECTOR_COLS = 384
+VECTOR_COLS = 392
 
 ROW_LAG = 4
 QK_LAG = 6

@@ -22,19 +22,20 @@ O_CHUNKS = O // P
 FLOPS = 2 * B * H * W * (2 * O * C + W * O)
 
 UNIT_ROWS = 8
-GROUP_ROWS = 4
 UNIT_COLS = UNIT_ROWS * W
-GROUP_COLS = GROUP_ROWS * W
 UNITS = [(b, half, side) for b in range(B) for half in range(H // UNIT_ROWS) for side in range(2)]
-GROUPS_PER_UNIT = UNIT_ROWS // GROUP_ROWS
-PIECES_PER_UNIT = C_PASSES * GROUPS_PER_UNIT
-N_PIECES = len(UNITS) * PIECES_PER_UNIT
-N_GROUPS = len(UNITS) * GROUPS_PER_UNIT
-N_ROWS = len(UNITS) * UNIT_ROWS
-ROWS_PER_STEP = N_ROWS // N_PIECES
+COARSE = ((0, 4), (4, 4))
+FINE = ((0, 4), (4, 2), (6, 2))
+GROUPS = [
+    (unit, first, rows)
+    for unit in range(len(UNITS))
+    for first, rows in (FINE if unit == len(UNITS) - 1 else COARSE)
+]
+N_GROUPS = len(GROUPS)
+N_PIECES = N_GROUPS * C_PASSES
 
 UNITS_AHEAD = 4
-VECTOR_COLS = 392
+SCALAR_COLS = {4: 120, 2: 32}
 
 ROW_LAG = 4
 QK_LAG = 6
@@ -70,6 +71,7 @@ def tile_sttm_single_pa_t_kernel(tc, left_feat, right_feat, wq, wk, out):
         qk_grouped = {}
         qk_codes = {}
         qk_scales = {}
+        q_place = {}
         dots = {}
 
         def load_feature(unit, g):
@@ -120,18 +122,17 @@ def tile_sttm_single_pa_t_kernel(tc, left_feat, right_feat, wq, wk, out):
             w_scales[side] = scales
 
         def piece_place(piece):
-            unit = piece // PIECES_PER_UNIT
-            part = (piece % PIECES_PER_UNIT) // C_PASSES
-            g = piece % C_PASSES
-            return unit, g, slice(part * GROUP_COLS, (part + 1) * GROUP_COLS)
+            unit, first, rows = GROUPS[piece // C_PASSES]
+            return unit, piece % C_PASSES, slice(first * W, (first + rows) * W), rows
 
         def regroup(piece):
-            unit, g, cols = piece_place(piece)
-            tile_g = grouped_pool.tile([P, GROUP_COLS, PACK], BF16, name="grouped", align_bytes=64)
+            unit, g, cols, rows = piece_place(piece)
+            tile_g = grouped_pool.tile([P, rows * W, PACK], BF16, name="grouped", align_bytes=64)
             src = raw[(unit, g)][:, :, cols]
+            vector_cols = rows * W - SCALAR_COLS[rows]
             for copy, share in (
-                (nc.vector.tensor_copy, slice(0, VECTOR_COLS)),
-                (nc.scalar.copy, slice(VECTOR_COLS, GROUP_COLS)),
+                (nc.vector.tensor_copy, slice(0, vector_cols)),
+                (nc.scalar.copy, slice(vector_cols, rows * W)),
             ):
                 copy(
                     out=tile_g[:, share, :].rearrange("p (c i) j -> p c j i", i=4),
@@ -140,8 +141,8 @@ def tile_sttm_single_pa_t_kernel(tc, left_feat, right_feat, wq, wk, out):
             grouped[piece] = tile_g
 
         def quantise(piece):
-            unit, g, cols = piece_place(piece)
-            if piece % PIECES_PER_UNIT == 0:
+            unit, g, cols, rows = piece_place(piece)
+            if g == 0 and cols.start == 0:
                 codes = f_pool.tile([P, C_PASSES, UNIT_COLS], U32, name="f_codes", align_bytes=64)
                 scales = f_pool.tile([P, C_PASSES, UNIT_COLS], U8, name="f_scales", align_bytes=64)
                 f_codes[unit] = codes
@@ -152,11 +153,10 @@ def tile_sttm_single_pa_t_kernel(tc, left_feat, right_feat, wq, wk, out):
                 in_=grouped[piece][:].rearrange("p w j -> p (w j)"),
             )
 
-        def project(row, copy_out):
-            unit = row // UNIT_ROWS
+        def project(group, r, copy_out):
+            unit, first, rows = GROUPS[group]
             side = UNITS[unit][2]
-            group = row // GROUP_ROWS
-            cols = slice((row % UNIT_ROWS) * W, (row % UNIT_ROWS + 1) * W)
+            cols = slice((first + r) * W, (first + r + 1) * W)
             acc = acc_pool.tile([P, O_CHUNKS, W], F32, name="acc", tag="acc")
             for t in range(O_CHUNKS):
                 for g in range(C_PASSES):
@@ -169,16 +169,15 @@ def tile_sttm_single_pa_t_kernel(tc, left_feat, right_feat, wq, wk, out):
                         start=(g == 0),
                         stop=(g == C_PASSES - 1),
                     )
-            if row % GROUP_ROWS == 0:
-                tile_g = qk_stage.tile([P, GROUP_ROWS, W, O_CHUNKS], BF16, name="qk_grouped", align_bytes=64)
+            if r == 0:
+                tile_g = qk_stage.tile([P, rows, W, O_CHUNKS], BF16, name="qk_grouped", align_bytes=64)
                 qk_grouped[group] = tile_g
-            copy_out(
-                out=qk_grouped[group][:, row % GROUP_ROWS, :, :], in_=acc[:].rearrange("p t w -> p w t")
-            )
+            copy_out(out=qk_grouped[group][:, r, :, :], in_=acc[:].rearrange("p t w -> p w t"))
 
         def quantise_qk(group):
-            codes = qk_pool.tile([P, GROUP_COLS], U32, name="qk_codes", align_bytes=64)
-            scales = qk_pool.tile([P, GROUP_COLS], U8, name="qk_scales", align_bytes=64)
+            unit, first, rows = GROUPS[group]
+            codes = qk_pool.tile([P, rows * W], U32, name="qk_codes", align_bytes=64)
+            scales = qk_pool.tile([P, rows * W], U8, name="qk_scales", align_bytes=64)
             nc.vector.quantize_mx(
                 out=codes[:].bitcast(FP8X4),
                 scales=scales[:],
@@ -186,34 +185,36 @@ def tile_sttm_single_pa_t_kernel(tc, left_feat, right_feat, wq, wk, out):
             )
             qk_codes[group] = codes
             qk_scales[group] = scales
+            for r in range(rows):
+                q_place[(unit, first + r)] = (group, slice(r * W, (r + 1) * W))
 
         def multiply_scores(k_group):
-            q_group = k_group - GROUPS_PER_UNIT
-            bank = dots_pool.tile([P, GROUP_ROWS, W], F32, name="dots")
-            for r in range(GROUP_ROWS):
-                cols = slice(r * W, (r + 1) * W)
+            unit, first, rows = GROUPS[k_group]
+            bank = dots_pool.tile([P, rows, W], F32, name="dots")
+            for r in range(rows):
+                q_group, q_cols = q_place[(unit - 1, first + r)]
+                k_cols = slice(r * W, (r + 1) * W)
                 nc.tensor.matmul_mx(
                     out=bank[:, r, :],
-                    lhsT=qk_codes[q_group][:, cols].bitcast(FP8X4),
-                    lhsT_scale=qk_scales[q_group][:, cols],
-                    rhs=qk_codes[k_group][:, cols].bitcast(FP8X4),
-                    rhs_scale=qk_scales[k_group][:, cols],
+                    lhsT=qk_codes[q_group][:, q_cols].bitcast(FP8X4),
+                    lhsT_scale=qk_scales[q_group][:, q_cols],
+                    rhs=qk_codes[k_group][:, k_cols].bitcast(FP8X4),
+                    rhs_scale=qk_scales[k_group][:, k_cols],
                     start=True,
                     stop=True,
                 )
             dots[k_group] = bank
 
         def store_scores(k_group):
-            b, half, side = UNITS[k_group // GROUPS_PER_UNIT]
-            first = half * UNIT_ROWS + (k_group % GROUPS_PER_UNIT) * GROUP_ROWS
-            res = res_pool.tile([P, GROUP_ROWS, W], F32, name="res")
+            unit, first, rows = GROUPS[k_group]
+            b, half, side = UNITS[unit]
+            row = half * UNIT_ROWS + first
+            res = res_pool.tile([P, rows, W], F32, name="res")
             nc.scalar.mul(out=res[:], in_=dots[k_group][:], mul=SCALE)
-            nc.sync.dma_start(
-                out=out[b, first : first + GROUP_ROWS, :, :].rearrange("h w x -> w h x"), in_=res[:]
-            )
+            nc.sync.dma_start(out=out[b, row : row + rows, :, :].rearrange("h w x -> w h x"), in_=res[:])
 
         def is_right(group):
-            return 0 <= group < N_GROUPS and UNITS[group // GROUPS_PER_UNIT][2] == 1
+            return 0 <= group < N_GROUPS and UNITS[GROUPS[group][0]][2] == 1
 
         for unit in range(UNITS_AHEAD):
             for g in range(C_PASSES):
@@ -232,18 +233,21 @@ def tile_sttm_single_pa_t_kernel(tc, left_feat, right_feat, wq, wk, out):
                 regroup(k)
             if 1 <= k <= N_PIECES:
                 quantise(k - 1)
-            next_unit = k // PIECES_PER_UNIT + UNITS_AHEAD - 1
-            if k % PIECES_PER_UNIT == 0 and UNITS_AHEAD <= next_unit < len(UNITS):
-                for g in range(C_PASSES):
-                    load_feature(next_unit, g)
+            if k < N_PIECES and k % C_PASSES == 0 and GROUPS[k // C_PASSES][1] == 0:
+                next_unit = GROUPS[k // C_PASSES][0] + UNITS_AHEAD - 1
+                if UNITS_AHEAD <= next_unit < len(UNITS):
+                    for g in range(C_PASSES):
+                        load_feature(next_unit, g)
             for side in range(2):
-                if k == side * PIECES_PER_UNIT + 2:
+                if k == side * len(COARSE) * C_PASSES + 2:
                     transpose_weight(side)
-                if k == side * PIECES_PER_UNIT + 3:
+                if k == side * len(COARSE) * C_PASSES + 3:
                     quantise_weight(side)
-            for row in range((k - ROW_LAG) * ROWS_PER_STEP, (k - ROW_LAG + 1) * ROWS_PER_STEP):
-                if 0 <= row < N_ROWS:
-                    project(row, nc.vector.tensor_copy if k > N_PIECES and row % 2 == 1 else nc.scalar.copy)
+            group, part = divmod(k - ROW_LAG, C_PASSES)
+            if 0 <= group < N_GROUPS:
+                half_rows = GROUPS[group][2] // 2
+                for r in range(part * half_rows, (part + 1) * half_rows):
+                    project(group, r, nc.vector.tensor_copy if k > N_PIECES and r % 2 == 1 else nc.scalar.copy)
             if (k - QK_LAG) % 2 == 0 and 0 <= (k - QK_LAG) // 2 < N_GROUPS:
                 quantise_qk((k - QK_LAG) // 2)
             if (k - SCORE_LAG) % 2 == 0 and is_right((k - SCORE_LAG) // 2):

@@ -35,7 +35,9 @@ N_GROUPS = len(GROUPS)
 N_PIECES = N_GROUPS * C_PASSES
 
 UNITS_AHEAD = 4
-SCALAR_COLS = {4: 120, 2: 32}
+HEAD_UNITS = 2
+HEAD_PIECES = HEAD_UNITS * len(COARSE) * C_PASSES
+SCALAR_COLS = {4: 128, 2: 32}
 
 ROW_LAG = 4
 QK_LAG = 6
@@ -52,6 +54,7 @@ def tile_sttm_single_pa_t_kernel(tc, left_feat, right_feat, wq, wk, out):
         consts = ctx.enter_context(tc.tile_pool(name="consts", bufs=1))
         w_stage = ctx.enter_context(tc.tile_pool(name="w_stage", bufs=2))
         raw_pool = ctx.enter_context(tc.tile_pool(name="raw", bufs=UNITS_AHEAD * C_PASSES))
+        head_pool = ctx.enter_context(tc.tile_pool(name="head", bufs=HEAD_PIECES))
         grouped_pool = ctx.enter_context(tc.tile_pool(name="grouped", bufs=3))
         f_pool = ctx.enter_context(tc.tile_pool(name="f_codes", bufs=3))
         qk_stage = ctx.enter_context(tc.tile_pool(name="qk_stage", bufs=3))
@@ -60,6 +63,7 @@ def tile_sttm_single_pa_t_kernel(tc, left_feat, right_feat, wq, wk, out):
         acc_pool = ctx.enter_context(tc.psum_pool(name="acc", bufs=6))
         dots_pool = ctx.enter_context(tc.psum_pool(name="dots", bufs=2))
 
+        head_raw = {}
         raw = {}
         w_raw = {}
         w_grouped = {}
@@ -84,6 +88,19 @@ def tile_sttm_single_pa_t_kernel(tc, left_feat, right_feat, wq, wk, out):
                 ].rearrange("(p j) h w -> p j (h w)", j=PACK),
             )
             raw[(unit, g)] = tile_raw
+
+        def load_head_piece(piece):
+            unit, g, cols, rows = piece_place(piece)
+            b, half, side = UNITS[unit]
+            row = half * UNIT_ROWS + cols.start // W
+            tile_raw = head_pool.tile([P, PACK, rows * W], BF16, name="raw_head")
+            nc.sync.dma_start(
+                out=tile_raw[:],
+                in_=feats[side][b, g * K_PASS : (g + 1) * K_PASS, row : row + rows, :].rearrange(
+                    "(p j) h w -> p j (h w)", j=PACK
+                ),
+            )
+            head_raw[piece] = tile_raw
 
         def load_weight(side):
             tile_w = w_stage.tile([P, O_CHUNKS * C], BF16, name="w_raw")
@@ -128,7 +145,7 @@ def tile_sttm_single_pa_t_kernel(tc, left_feat, right_feat, wq, wk, out):
         def regroup(piece):
             unit, g, cols, rows = piece_place(piece)
             tile_g = grouped_pool.tile([P, rows * W, PACK], BF16, name="grouped", align_bytes=64)
-            src = raw[(unit, g)][:, :, cols]
+            src = head_raw[piece][:] if piece in head_raw else raw[(unit, g)][:, :, cols]
             vector_cols = rows * W - SCALAR_COLS[rows]
             for copy, share in (
                 (nc.vector.tensor_copy, slice(0, vector_cols)),
@@ -216,11 +233,14 @@ def tile_sttm_single_pa_t_kernel(tc, left_feat, right_feat, wq, wk, out):
         def is_right(group):
             return 0 <= group < N_GROUPS and UNITS[GROUPS[group][0]][2] == 1
 
-        for unit in range(UNITS_AHEAD):
+        for item in (-1, 0, 1, 2, 3, -2, 4, 5, 6, 7):
+            if item < 0:
+                load_weight(-item - 1)
+            else:
+                load_head_piece(item)
+        for unit in range(HEAD_UNITS, HEAD_UNITS + UNITS_AHEAD):
             for g in range(C_PASSES):
                 load_feature(unit, g)
-            if unit < 2:
-                load_weight(unit)
 
         ident = consts.tile([P, P], F32, name="ident")
         make_identity(nc, ident[:])
@@ -229,20 +249,20 @@ def tile_sttm_single_pa_t_kernel(tc, left_feat, right_feat, wq, wk, out):
         nc.scalar.mul(out=warm[:], in_=warm[:], mul=SCALE)
 
         for k in range(N_PIECES + STORE_LAG):
+            for side, t_step, q_step in ((0, 0, 2), (1, 4, 6)):
+                if k == t_step:
+                    transpose_weight(side)
+                if k == q_step:
+                    quantise_weight(side)
             if k < N_PIECES:
                 regroup(k)
             if 1 <= k <= N_PIECES:
                 quantise(k - 1)
             if k < N_PIECES and k % C_PASSES == 0 and GROUPS[k // C_PASSES][1] == 0:
                 next_unit = GROUPS[k // C_PASSES][0] + UNITS_AHEAD - 1
-                if UNITS_AHEAD <= next_unit < len(UNITS):
+                if HEAD_UNITS + UNITS_AHEAD <= next_unit < len(UNITS):
                     for g in range(C_PASSES):
                         load_feature(next_unit, g)
-            for side in range(2):
-                if k == side * len(COARSE) * C_PASSES + 2:
-                    transpose_weight(side)
-                if k == side * len(COARSE) * C_PASSES + 3:
-                    quantise_weight(side)
             group, part = divmod(k - ROW_LAG, C_PASSES)
             if 0 <= group < N_GROUPS:
                 half_rows = GROUPS[group][2] // 2

from contextlib import ExitStack

import concourse.mybir as mybir
from concourse.masks import make_identity

F32 = mybir.dt.float32
BF16 = mybir.dt.bfloat16
U32 = mybir.dt.uint32
U8 = mybir.dt.uint8
FP8X4 = mybir.dt.float8_e4m3fn_x4

B, C, H, W = 2, 1024, 16, 128
O = 512
SCALE = 0.125

P = 128
PACK = 4
K_PASS = P * PACK
C_PASSES = C // K_PASS
O_CHUNKS = O // P

FLOPS = 2 * B * H * W * (2 * O * C + W * O)

UNIT_ROWS = 8
UNIT_COLS = UNIT_ROWS * W
UNITS = [(b, half, side) for b in range(B) for half in range(H // UNIT_ROWS) for side in range(2)]
COARSE = ((0, 4), (4, 4))
FINE = ((0, 4), (4, 2), (6, 2))
GROUPS = [
    (unit, first, rows)
    for unit in range(len(UNITS))
    for first, rows in (FINE if unit == len(UNITS) - 1 else COARSE)
]
N_GROUPS = len(GROUPS)
N_PIECES = N_GROUPS * C_PASSES

UNITS_AHEAD = 4
HEAD_UNITS = 2
HEAD_PIECES = HEAD_UNITS * len(COARSE) * C_PASSES
SCALAR_COLS = {4: 128, 2: 32}

ROW_LAG = 4
QK_LAG = 6
SCORE_LAG = 7
STORE_LAG = 8


def tile_sttm_single_pa_t_kernel(tc, left_feat, right_feat, wq, wk, out):
    nc = tc.nc
    feats = (left_feat, right_feat)
    weights = (wq, wk)

    with ExitStack() as ctx:
        consts = ctx.enter_context(tc.tile_pool(name="consts", bufs=1))
        w_stage = ctx.enter_context(tc.tile_pool(name="w_stage", bufs=2))
        raw_pool = ctx.enter_context(tc.tile_pool(name="raw", bufs=UNITS_AHEAD * C_PASSES))
        head_pool = ctx.enter_context(tc.tile_pool(name="head", bufs=HEAD_PIECES))
        grouped_pool = ctx.enter_context(tc.tile_pool(name="grouped", bufs=3))
        f_pool = ctx.enter_context(tc.tile_pool(name="f_codes", bufs=3))
        qk_stage = ctx.enter_context(tc.tile_pool(name="qk_stage", bufs=3))
        qk_pool = ctx.enter_context(tc.tile_pool(name="qk_codes", bufs=6))
        res_pool = ctx.enter_context(tc.tile_pool(name="res", bufs=3))
        acc_pool = ctx.enter_context(tc.psum_pool(name="acc", bufs=6))
        dots_pool = ctx.enter_context(tc.psum_pool(name="dots", bufs=2))

        head_raw = {}
        raw = {}
        w_raw = {}
        w_grouped = {}
        w_codes = {}
        w_scales = {}
        grouped = {}
        f_codes = {}
        f_scales = {}
        qk_grouped = {}
        qk_codes = {}
        qk_scales = {}
        q_place = {}
        dots = {}

        def load_feature(unit, g):
            b, half, side = UNITS[unit]
            tile_raw = raw_pool.tile([P, PACK, UNIT_COLS], BF16, name="raw")
            nc.sync.dma_start(
                out=tile_raw[:],
                in_=feats[side][
                    b, g * K_PASS : (g + 1) * K_PASS, half * UNIT_ROWS : (half + 1) * UNIT_ROWS, :
                ].rearrange("(p j) h w -> p j (h w)", j=PACK),
            )
            raw[(unit, g)] = tile_raw

        def load_head_piece(piece):
            unit, g, cols, rows = piece_place(piece)
            b, half, side = UNITS[unit]
            row = half * UNIT_ROWS + cols.start // W
            tile_raw = head_pool.tile([P, PACK, rows * W], BF16, name="raw_head")
            nc.sync.dma_start(
                out=tile_raw[:],
                in_=feats[side][b, g * K_PASS : (g + 1) * K_PASS, row : row + rows, :].rearrange(
                    "(p j) h w -> p j (h w)", j=PACK
                ),
            )
            head_raw[piece] = tile_raw

        def load_weight(side):
            tile_w = w_stage.tile([P, O_CHUNKS * C], BF16, name="w_raw")
            nc.sync.dma_start(
                out=tile_w[:], in_=weights[side].rearrange("(m t) c -> m (t c)", t=O_CHUNKS)
            )
            w_raw[side] = tile_w

        def transpose_weight(side):
            words = w_raw[side][:].bitcast(F32).rearrange(
                "m (t g p u) -> m t g u p", t=O_CHUNKS, g=C_PASSES, p=P, u=2
            )
            tile_g = w_stage.tile([P, C_PASSES * O_CHUNKS * P * PACK], BF16, name="w_grouped", align_bytes=64)
            grouped_words = tile_g[:].bitcast(F32).rearrange(
                "p (g t m u) -> p g t m u", g=C_PASSES, t=O_CHUNKS, m=P, u=2
            )
            for t in range(O_CHUNKS):
                flipped = acc_pool.tile([P, C_PASSES, 2, P], F32, name="flipped", tag="acc")
                for g in range(C_PASSES):
                    for u in range(2):
                        nc.tensor.transpose(flipped[:, g, u, :], words[:, t, g, u, :], ident[:])
                nc.scalar.copy(
                    out=grouped_words[:, :, t, :, :], in_=flipped[:].rearrange("p g u m -> p g m u")
                )
            w_grouped[side] = tile_g

        def quantise_weight(side):
            codes = consts.tile([P, C_PASSES, O_CHUNKS, P], U32, name="w_codes%d" % side, align_bytes=64)
            scales = consts.tile([P, C_PASSES, O_CHUNKS, P], U8, name="w_scales%d" % side, align_bytes=64)
            nc.vector.quantize_mx(
                out=codes[:].rearrange("p g t m -> p (g t m)").bitcast(FP8X4),
                scales=scales[:].rearrange("p g t m -> p (g t m)"),
                in_=w_grouped[side][:],
            )
            w_codes[side] = codes
            w_scales[side] = scales

        def piece_place(piece):
            unit, first, rows = GROUPS[piece // C_PASSES]
            return unit, piece % C_PASSES, slice(first * W, (first + rows) * W), rows

        def regroup(piece):
            unit, g, cols, rows = piece_place(piece)
            tile_g = grouped_pool.tile([P, rows * W, PACK], BF16, name="grouped", align_bytes=64)
            src = head_raw[piece][:] if piece in head_raw else raw[(unit, g)][:, :, cols]
            vector_cols = rows * W - SCALAR_COLS[rows]
            for copy, share in (
                (nc.vector.tensor_copy, slice(0, vector_cols)),
                (nc.scalar.copy, slice(vector_cols, rows * W)),
            ):
                copy(
                    out=tile_g[:, share, :].rearrange("p (c i) j -> p c j i", i=4),
                    in_=src[:, :, share].rearrange("p j (c i) -> p c j i", i=4),
                )
            grouped[piece] = tile_g

        def quantise(piece):
            unit, g, cols, rows = piece_place(piece)
            if g == 0 and cols.start == 0:
                codes = f_pool.tile([P, C_PASSES, UNIT_COLS], U32, name="f_codes", align_bytes=64)
                scales = f_pool.tile([P, C_PASSES, UNIT_COLS], U8, name="f_scales", align_bytes=64)
                f_codes[unit] = codes
                f_scales[unit] = scales
            nc.vector.quantize_mx(
                out=f_codes[unit][:, g, cols].bitcast(FP8X4),
                scales=f_scales[unit][:, g, cols],
                in_=grouped[piece][:].rearrange("p w j -> p (w j)"),
            )

        def project(group, r, copy_out):
            unit, first, rows = GROUPS[group]
            side = UNITS[unit][2]
            cols = slice((first + r) * W, (first + r + 1) * W)
            acc = acc_pool.tile([P, O_CHUNKS, W], F32, name="acc", tag="acc")
            for t in range(O_CHUNKS):
                for g in range(C_PASSES):
                    nc.tensor.matmul_mx(
                        out=acc[:, t, :],
                        lhsT=w_codes[side][:, g, t, :].bitcast(FP8X4),
                        lhsT_scale=w_scales[side][:, g, t, :],
                        rhs=f_codes[unit][:, g, cols].bitcast(FP8X4),
                        rhs_scale=f_scales[unit][:, g, cols],
                        start=(g == 0),
                        stop=(g == C_PASSES - 1),
                    )
            if r == 0:
                tile_g = qk_stage.tile([P, rows, W, O_CHUNKS], BF16, name="qk_grouped", align_bytes=64)
                qk_grouped[group] = tile_g
            copy_out(out=qk_grouped[group][:, r, :, :], in_=acc[:].rearrange("p t w -> p w t"))

        def quantise_qk(group):
            unit, first, rows = GROUPS[group]
            codes = qk_pool.tile([P, rows * W], U32, name="qk_codes", align_bytes=64)
            scales = qk_pool.tile([P, rows * W], U8, name="qk_scales", align_bytes=64)
            nc.vector.quantize_mx(
                out=codes[:].bitcast(FP8X4),
                scales=scales[:],
                in_=qk_grouped[group][:].rearrange("p r w t -> p (r w t)"),
            )
            qk_codes[group] = codes
            qk_scales[group] = scales
            for r in range(rows):
                q_place[(unit, first + r)] = (group, slice(r * W, (r + 1) * W))

        def multiply_scores(k_group):
            unit, first, rows = GROUPS[k_group]
            bank = dots_pool.tile([P, rows, W], F32, name="dots")
            for r in range(rows):
                q_group, q_cols = q_place[(unit - 1, first + r)]
                k_cols = slice(r * W, (r + 1) * W)
                nc.tensor.matmul_mx(
                    out=bank[:, r, :],
                    lhsT=qk_codes[q_group][:, q_cols].bitcast(FP8X4),
                    lhsT_scale=qk_scales[q_group][:, q_cols],
                    rhs=qk_codes[k_group][:, k_cols].bitcast(FP8X4),
                    rhs_scale=qk_scales[k_group][:, k_cols],
                    start=True,
                    stop=True,
                )
            dots[k_group] = bank

        def store_scores(k_group):
            unit, first, rows = GROUPS[k_group]
            b, half, side = UNITS[unit]
            row = half * UNIT_ROWS + first
            res = res_pool.tile([P, rows, W], F32, name="res")
            nc.scalar.mul(out=res[:], in_=dots[k_group][:], mul=SCALE)
            nc.sync.dma_start(out=out[b, row : row + rows, :, :].rearrange("h w x -> w h x"), in_=res[:])

        def is_right(group):
            return 0 <= group < N_GROUPS and UNITS[GROUPS[group][0]][2] == 1

        for item in (-1, 0, 1, 2, 3, -2, 4, 5, 6, 7):
            if item < 0:
                load_weight(-item - 1)
            else:
                load_head_piece(item)
        for unit in range(HEAD_UNITS, HEAD_UNITS + UNITS_AHEAD):
            for g in range(C_PASSES):
                load_feature(unit, g)

        ident = consts.tile([P, P], F32, name="ident")
        make_identity(nc, ident[:])
        warm = consts.tile([P, 1], F32, name="warm")
        nc.vector.memset(warm[:], 0.0)
        nc.scalar.mul(out=warm[:], in_=warm[:], mul=SCALE)

        for k in range(N_PIECES + STORE_LAG):
            for side, t_step, q_step in ((0, 0, 2), (1, 4, 6)):
                if k == t_step:
                    transpose_weight(side)
                if k == q_step:
                    quantise_weight(side)
            if k < N_PIECES:
                regroup(k)
            if 1 <= k <= N_PIECES:
                quantise(k - 1)
            if k < N_PIECES and k % C_PASSES == 0 and GROUPS[k // C_PASSES][1] == 0:
                next_unit = GROUPS[k // C_PASSES][0] + UNITS_AHEAD - 1
                if HEAD_UNITS + UNITS_AHEAD <= next_unit < len(UNITS):
                    for g in range(C_PASSES):
                        load_feature(next_unit, g)
            group, part = divmod(k - ROW_LAG, C_PASSES)
            if 0 <= group < N_GROUPS:
                half_rows = GROUPS[group][2] // 2
                for r in range(part * half_rows, (part + 1) * half_rows):
                    project(group, r, nc.vector.tensor_copy if k > N_PIECES and r % 2 == 1 else nc.scalar.copy)
            if (k - QK_LAG) % 2 == 0 and 0 <= (k - QK_LAG) // 2 < N_GROUPS:
                quantise_qk((k - QK_LAG) // 2)
            if (k - SCORE_LAG) % 2 == 0 and is_right((k - SCORE_LAG) // 2):
                multiply_scores((k - SCORE_LAG) // 2)
            if (k - STORE_LAG) % 2 == 0 and is_right((k - STORE_LAG) // 2):
                store_scores((k - STORE_LAG) // 2)
